import numpy as np
import ml_dtypes


def mxq(x, axis, fmt="e4m3"):
    dtype, down = {"e4m3": (ml_dtypes.float8_e4m3fn, 7), "e5m2": (ml_dtypes.float8_e5m2, 14)}[fmt]
    v = np.moveaxis(np.asarray(x, np.float32).astype(ml_dtypes.bfloat16).astype(np.float64), axis, -1)
    blocks = v.reshape(v.shape[:-1] + (-1, 32))
    amax = np.abs(blocks).max(-1, keepdims=True)
    byte = np.maximum(np.where(amax > 0, np.frexp(amax)[1] - 1 + 127, 0) - down, 1)
    scale = np.exp2(byte - 127.0)
    codes = (blocks / scale).astype(np.float32).astype(dtype).astype(np.float64)
    return np.moveaxis((codes * scale).reshape(v.shape), -1, axis)


WIDE = False


def mx_kscale(k):
    if not WIDE:
        return np.ones(k)
    levels = np.array([10, -10, 5, -5, 0])
    a = np.random.permutation(np.resize(levels, k // 512 * 4)).reshape(k // 512, 4)
    idx = np.arange(k)
    return np.exp2(a[idx // 512, idx % 128 // 32])


BF16 = ml_dtypes.bfloat16


def bf(x):
    return np.asarray(x, np.float32).astype(BF16)


def f64(x):
    return np.asarray(x).astype(np.float64)


B, G, C0, C1, C2, NO = 4, 32, 1024, 1024, 1024, 128
G0, G1, G2 = G, G // 2, G // 4
STRIDES = (8.0, 16.0, 32.0)


def sigmoid(v):
    return 1.0 / (1.0 + np.exp(-v))


def decode_level(feat, W, b, stride, level):
    bs, _, ny, nx = feat.shape
    p = (mxq(feat, 1, "e4m3").transpose(0, 2, 3, 1) @ mxq(W, 1, "e4m3").T) + b
    y = sigmoid(p)
    xv = np.arange(nx, dtype=np.float64)
    yv = np.arange(ny, dtype=np.float64)[:, None]
    power = 2.0 ** level
    d = (y[..., :4] * 2.0) ** 2 * power
    x1 = (xv + 1.0 - d[..., 0]) * stride
    y1 = (yv + 1.0 - d[..., 1]) * stride
    x2 = (xv + d[..., 2]) * stride
    y2 = (yv + d[..., 3]) * stride
    box = np.stack([(x1 + x2) * 0.5, (y1 + y2) * 0.5, x2 - x1, y2 - y1], axis=-1)
    out = np.concatenate([box, y[..., 4:]], axis=-1)
    return out.reshape(bs, ny * nx, out.shape[-1])


def setup_inputs():
    s0, s1, s2 = mx_kscale(C0), mx_kscale(C1), mx_kscale(C2)
    return {
        "x0": bf(np.random.standard_normal((B, C0, G0, G0)) * s0[None, :, None, None]),
        "x1": bf(np.random.standard_normal((B, C1, G1, G1)) * s1[None, :, None, None]),
        "x2": bf(np.random.standard_normal((B, C2, G2, G2)) * s2[None, :, None, None]),
        "W0": bf(np.random.standard_normal((NO, C0)) / np.sqrt(C0) / s0),
        "b0": bf(np.random.standard_normal(NO) * 0.5),
        "W1": bf(np.random.standard_normal((NO, C1)) / np.sqrt(C1) / s1),
        "b1": bf(np.random.standard_normal(NO) * 0.5),
        "W2": bf(np.random.standard_normal((NO, C2)) / np.sqrt(C2) / s2),
        "b2": bf(np.random.standard_normal(NO) * 0.5),
    }


def reference(x0, x1, x2, W0, b0, W1, b1, W2, b2):
    feats = (f64(x0), f64(x1), f64(x2))
    Ws = (f64(W0), f64(W1), f64(W2))
    bs_ = (f64(b0), f64(b1), f64(b2))
    z = [decode_level(feats[i], Ws[i], bs_[i], STRIDES[i], i) for i in range(3)]
    return np.concatenate(z, axis=1)

@@ -1,0 +1,402 @@
+from contextlib import ExitStack
+
+import concourse.mybir as mybir
+from concourse.masks import make_identity
+
+FLOPS = 2 * 4 * 1344 * 1024 * 128
+
+BF16 = mybir.dt.bfloat16
+F32 = mybir.dt.float32
+I32 = mybir.dt.int32
+U32 = mybir.dt.uint32
+U8 = mybir.dt.uint8
+FP8X4 = mybir.dt.float8_e4m3fn_x4
+ALU = mybir.AluOpType
+ACT = mybir.ActivationFunctionType
+
+P = 128
+MANUAL = False
+WV0 = 648
+
+
+def tile_objectboxdetect_t_kernel(tc, x0, x1, x2, W0, b0, W1, b1, W2, b2, out):
+    nc = tc.nc
+    weights = (W0, W1, W2)
+    biases = (b0, b1, b2)
+    with ExitStack() as ctx:
+        if MANUAL:
+            ctx.enter_context(tc.manual_schedule())
+        const = ctx.enter_context(tc.tile_pool(name="const", bufs=1))
+        rawp = ctx.enter_context(tc.tile_pool(name="raw", bufs=1))
+        grpp = ctx.enter_context(tc.tile_pool(name="grp", bufs=4))
+        codep = ctx.enter_context(tc.tile_pool(name="code", bufs=6))
+        yp = ctx.enter_context(tc.tile_pool(name="y", bufs=3))
+        outp = ctx.enter_context(tc.tile_pool(name="o", bufs=1))
+        small = ctx.enter_context(tc.tile_pool(name="small", bufs=3))
+        psum = ctx.enter_context(tc.psum_pool(name="psum", bufs=4))
+
+        x1src = {}
+        x0src = {}
+        x2src = {}
+        wraw = {}
+
+        def load_x1_half(n, c):
+            t = rawp.tile([P, 4, 256], BF16, name="x1_%d_%d" % (n, c))
+            nc.sync.dma_start(
+                out=t[:].rearrange("p j w -> p (j w)"),
+                in_=x1[n, 512 * c : 512 * (c + 1)].rearrange("(p j) h w -> p (j h w)", j=4),
+            )
+            x1src[(n, c)] = t[:]
+
+        def load_x1(n):
+            t = rawp.tile([P, 2, 4, 256], BF16, name="x1_%d" % n)
+            nc.sync.dma_start(
+                out=t[:].rearrange("p c j w -> p c (j w)"),
+                in_=x1[n].rearrange("(c p j) h w -> p c (j h w)", c=2, j=4),
+            )
+            x1src[(n, 0)] = t[:, 0]
+            x1src[(n, 1)] = t[:, 1]
+
+        def load_x0(n, c):
+            t = rawp.tile([P, 4, 1024], BF16, name="x0_%d_%d" % (n, c))
+            nc.sync.dma_start(
+                out=t[:].rearrange("p j w -> p (j w)"),
+                in_=x0[n, 512 * c : 512 * (c + 1)].rearrange("(p j) h w -> p (j h w)", j=4),
+            )
+            x0src[(n, c)] = t[:]
+
+        def load_x2(c):
+            t = rawp.tile([P, 4, 4, 64], BF16, name="x2_%d" % c)
+            nc.sync.dma_start(
+                out=t[:].rearrange("p n j w -> p n (j w)"),
+                in_=x2[:, 512 * c : 512 * (c + 1)].rearrange("n (p j) h w -> p n (j h w)", j=4),
+            )
+            x2src[c] = t[:]
+
+        def load_w(lvl):
+            t = rawp.tile([P, 1024], BF16, name="w_%d" % lvl)
+            nc.sync.dma_start(out=t[:], in_=weights[lvl][:, :])
+            wraw[lvl] = t
+
+        load_x1_half(0, 0)
+        load_w(1)
+        load_x1_half(0, 1)
+        load_x1(1)
+        load_x0(0, 0)
+        load_w(0)
+        load_x0(0, 1)
+        load_x0(1, 0)
+        load_w(2)
+        load_x0(1, 1)
+        for n in range(2, 4):
+            load_x0(n, 0)
+            load_x0(n, 1)
+        load_x1(2)
+        load_x1(3)
+        load_x2(0)
+        load_x2(1)
+
+        bias_bf = []
+        with nc.allow_non_contiguous_dma(reason="128 two-byte values, one a partition"):
+            for lvl in range(3):
+                t = const.tile([P, 1], BF16, name="bias_bf_%d" % lvl)
+                nc.scalar.dma_start(out=t[:], in_=biases[lvl].rearrange("(p o) -> p o", o=1))
+                bias_bf.append(t)
+
+        warm = const.tile([P, 1], F32, name="warm")
+        nc.vector.memset(warm[:], 0.0)
+        warm2 = const.tile([P, 1], F32, name="warm2")
+        nc.scalar.activation(out=warm2[:], in_=warm[:], func=ACT.Sigmoid)
+
+        idx = const.tile([P, 14], I32, name="idx")
+        nc.gpsimd.iota(idx[:, 0:8], pattern=[[1, 8]], base=0, channel_multiplier=8)
+        nc.gpsimd.iota(idx[:, 8:12], pattern=[[0, 2], [1, 2]], base=0, channel_multiplier=2)
+        nc.gpsimd.iota(idx[:, 12:14], pattern=[[0, 2]], base=0, channel_multiplier=1)
+        ident = const.tile([P, P], F32, name="ident")
+        make_identity(nc, ident[:])
+
+        gint = const.tile([P, 14, 2], I32, name="gint")
+        grid = const.tile([P, 14, 2], F32, name="grid")
+        slots = ((0, 8), (8, 12), (12, 14))
+        bits = (
+            ((31, ALU.logical_shift_left, 3), (0x3E0, ALU.logical_shift_right, 2)),
+            ((15, ALU.logical_shift_left, 4), (0xF0, ALU.logical_shift_left, 0)),
+            ((7, ALU.logical_shift_left, 5), (56, ALU.logical_shift_left, 2)),
+        )
+        for lvl in range(3):
+            lo, hi = slots[lvl]
+            for axis in range(2):
+                mask, shift_op, shift = bits[lvl][axis]
+                nc.vector.tensor_scalar(
+                    out=gint[:, lo:hi, axis],
+                    in0=idx[:, lo:hi],
+                    scalar1=mask,
+                    scalar2=shift,
+                    op0=ALU.bitwise_and,
+                    op1=shift_op,
+                )
+            nc.vector.tensor_scalar(
+                out=grid[:, lo:hi, :],
+                in0=gint[:, lo:hi, :],
+                scalar1=float(4 << lvl),
+                scalar2=None,
+                op0=ALU.add,
+            )
+
+        bias = const.tile([P, 3], F32, name="bias")
+        wcodes = {}
+        wscales = {}
+        wgrouped = {}
+
+        def wprep_a(lvl):
+            nc.vector.tensor_copy(out=bias[:, lvl : lvl + 1], in_=bias_bf[lvl][:])
+            words = wraw[lvl][:].bitcast(F32).rearrange("o (c p u) -> o c u p", c=2, u=2)
+            wt = psum.tile([P, 2, 2, P], F32, tag="zt")
+            for c in range(2):
+                for u in range(2):
+                    nc.tensor.transpose(wt[:, c, u, :], words[:, c, u, :], ident[:])
+            wg = const.tile([P, 1024], BF16, name="wg_%d" % lvl, align_bytes=64)
+            nc.scalar.copy(
+                out=wg[:].bitcast(F32).rearrange("p (c o u) -> p c o u", c=2, u=2),
+                in_=wt[:].rearrange("p c u o -> p c o u"),
+            )
+            wgrouped[lvl] = wg
+
+        def wprep_b(lvl):
+            wc = const.tile([P, 256], U32, name="wc_%d" % lvl, align_bytes=64)
+            ws = const.tile([P, 256], U8, name="ws_%d" % lvl, align_bytes=64)
+            nc.vector.quantize_mx(out=wc[:].bitcast(FP8X4), scales=ws[:], in_=wgrouped[lvl][:])
+            wcodes[lvl] = wc
+            wscales[lvl] = ws
+
+        def regroup(dst, src, wv):
+            width = dst.shape[1]
+            if wv > 0:
+                nc.vector.tensor_copy(
+                    out=dst[:, 0:wv, :].rearrange("p (c i) t -> p c t i", i=4),
+                    in_=src[:, :, 0:wv].rearrange("p t (c i) -> p c t i", i=4),
+                )
+            if wv < width:
+                nc.scalar.copy(
+                    out=dst[:, wv:width, :].rearrange("p (c i) t -> p c t i", i=4),
+                    in_=src[:, :, wv:width].rearrange("p t (c i) -> p c t i", i=4),
+                )
+
+        def stage_r(u, k):
+            words, subs = u["chunks"][k]
+            grp = grpp.tile([P, 1024, 4], BF16, tag="grp", align_bytes=64)
+            for lo, width, src, wv in subs:
+                regroup(grp[:, lo : lo + width, :], src, wv)
+            u["grp"][k] = grp
+
+        def stage_r_x2(u, k):
+            grp = grpp.tile([P, 1024, 4], BF16, tag="grp", align_bytes=64)
+            nc.vector.tensor_copy(
+                out=grp[:, 0:256, :].rearrange("p (n c i) t -> p n c t i", n=4, i=4),
+                in_=x2src[0].rearrange("p n t (c i) -> p n c t i", i=4),
+            )
+            nc.vector.tensor_copy(
+                out=grp[:, 256:384, :].rearrange("p (n c i) t -> p n c t i", n=2, i=4),
+                in_=x2src[1][:, 0:2].rearrange("p n t (c i) -> p n c t i", i=4),
+            )
+            nc.scalar.copy(
+                out=grp[:, 384:512, :].rearrange("p (n w) t -> p n w t", n=2),
+                in_=x2src[1][:, 2:4].rearrange("p n t w -> p n w t"),
+            )
+            u["grp"][k] = grp
+
+        def stage_q(u, k):
+            words = u["chunks"][k][0]
+            lvl = u["lvl"]
+            codes = codep.tile([P, 1024], U32, tag="codes", align_bytes=64)
+            scl = codep.tile([P, 1024], U8, tag="scl", align_bytes=64)
+            nc.vector.quantize_mx(
+                out=codes[:, 0:words].bitcast(FP8X4),
+                scales=scl[:, 0:words],
+                in_=u["grp"][k][:, 0:words, :].rearrange("p w t -> p (w t)"),
+            )
+            for bank, c, lo, cols in u["mx"][k]:
+                if c == 0:
+                    acc = psum.tile([P, 512], F32, tag="acc")
+                    u["acc"][bank] = acc
+                nc.tensor.matmul_mx(
+                    out=u["acc"][bank][:, 0:cols],
+                    lhsT=wcodes[lvl][:, P * c : P * (c + 1)].bitcast(FP8X4),
+                    lhsT_scale=wscales[lvl][:, P * c : P * (c + 1)],
+                    rhs=codes[:, lo : lo + cols].bitcast(FP8X4),
+                    rhs_scale=scl[:, lo : lo + cols],
+                    start=(c == 0),
+                    stop=(c == 1),
+                )
+
+        def stage_sg(u):
+            lvl = u["lvl"]
+            y = yp.tile([P, 8, P], F32, tag="y")
+            u["y"] = y
+            for bank in sorted(u["acc"]):
+                acc = u["acc"][bank]
+                if lvl == 0:
+                    dst = y[:, :, 64 * bank : 64 * bank + 64]
+                    src = acc[:].rearrange("o (m t) -> o t m", t=8)
+                elif lvl == 1:
+                    dst = y[:, 0:4, :].rearrange("o (n t) m -> o n t m", n=2)
+                    src = acc[:].rearrange("o (n m t) -> o n t m", n=2, t=2)
+                else:
+                    dst = y[:, 0:2, :].rearrange("o g m -> o (g m)")
+                    src = acc[:, 0:256]
+                nc.scalar.activation(
+                    out=dst, in_=src, func=ACT.Sigmoid, bias=bias[:, lvl : lvl + 1], scale=1.0
+                )
+
+        def stage_tr(u):
+            u["zt"] = []
+            per = u["per_bank"]
+            for g in range(u["nt"] // per):
+                zt = psum.tile([P, 4, P], F32, tag="zt")
+                for s in range(per):
+                    nc.tensor.transpose(zt[:, s, :], u["y"][:, per * g + s, :], ident[:])
+                u["zt"].append(zt)
+
+        def stage_ev(u):
+            per = u["per_bank"]
+            o = outp.tile([P, u["nt"], P], F32, name="o_" + u["name"])
+            u["o"] = o
+            for g, zt in enumerate(u["zt"]):
+                if u["ev"][g] == "v":
+                    nc.vector.tensor_copy(out=o[:, per * g : per * (g + 1), :], in_=zt[:, 0:per, :])
+                else:
+                    nc.scalar.copy(out=o[:, per * g : per * (g + 1), :], in_=zt[:, 0:per, :])
+
+        def stage_bx(u):
+            lvl = u["lvl"]
+            nt = u["nt"]
+            o = u["o"]
+            lo = slots[lvl][0]
+            stride = float(8 << lvl)
+            power = float(1 << lvl)
+            q = small.tile([P, 8, 4], F32, tag="q")
+            d = small.tile([P, 8, 2], F32, tag="d")
+            s = small.tile([P, 8, 2], F32, tag="s")
+            nc.vector.tensor_tensor(out=q[:, 0:nt, :], in0=o[:, :, 0:4], in1=o[:, :, 0:4], op=ALU.mult)
+            nc.vector.tensor_tensor(
+                out=d[:, 0:nt, :], in0=q[:, 0:nt, 2:4], in1=q[:, 0:nt, 0:2], op=ALU.subtract
+            )
+            nc.vector.tensor_tensor(
+                out=s[:, 0:nt, :], in0=q[:, 0:nt, 2:4], in1=q[:, 0:nt, 0:2], op=ALU.add
+            )
+            nc.vector.scalar_tensor_tensor(
+                out=o[:, :, 0:2],
+                in0=d[:, 0:nt, :],
+                scalar=2.0 * power * stride,
+                in1=grid[:, lo : lo + nt, :],
+                op0=ALU.mult,
+                op1=ALU.add,
+            )
+            nc.vector.tensor_scalar(
+                out=o[:, :, 2:4],
+                in0=s[:, 0:nt, :],
+                scalar1=4.0 * power * stride,
+                scalar2=-stride,
+                op0=ALU.mult,
+                op1=ALU.add,
+            )
+
+        def stage_st(u):
+            o = u["o"]
+            lvl = u["lvl"]
+            if lvl == 0:
+                nc.sync.dma_start(
+                    out=out[u["n"], 0:1024, :].rearrange("(m t) o -> m (t o)", t=8),
+                    in_=o[:].rearrange("m t o -> m (t o)"),
+                )
+            elif lvl == 1:
+                n = u["n"]
+                nc.sync.dma_start(
+                    out=out[n : n + 2, 1024:1280, :].rearrange("n (m t) o -> m n (t o)", t=2),
+                    in_=o[:].rearrange("m (n t) o -> m n (t o)", n=2),
+                )
+            else:
+                for n in range(4):
+                    half = 64 * (n % 2)
+                    nc.sync.dma_start(out=out[n, 1280:1344, :], in_=o[half : half + 64, n // 2, :])
+
+        def unit_x0(n):
+            return {
+                "name": "b%d" % n,
+                "lvl": 0,
+                "n": n,
+                "chunks": [(1024, [(0, 1024, x0src[(n, c)], WV0)]) for c in range(2)],
+                "mx": [[(h, c, 512 * h, 512) for h in range(2)] for c in range(2)],
+                "nt": 8,
+                "per_bank": 4,
+                "ev": ["s", "s"],
+                "grp": {},
+                "acc": {},
+            }
+
+        def unit_x1(h, wvs):
+            subs = []
+            for c in range(2):
+                for k in range(2):
+                    subs.append((512 * c + 256 * k, 256, x1src[(2 * h + k, c)], wvs[2 * c + k]))
+            return {
+                "name": "l1%d" % h,
+                "lvl": 1,
+                "n": 2 * h,
+                "chunks": [(1024, subs)],
+                "mx": [[(0, c, 512 * c, 512) for c in range(2)]],
+                "nt": 4,
+                "per_bank": 4,
+                "ev": ["s"],
+                "grp": {},
+                "acc": {},
+            }
+
+        def unit_x2():
+            return {
+                "name": "l2",
+                "lvl": 2,
+                "n": 0,
+                "chunks": [(512, None)],
+                "mx": [[(0, c, 256 * c, 256) for c in range(2)]],
+                "nt": 2,
+                "per_bank": 1,
+                "ev": ["v", "s"],
+                "grp": {},
+                "acc": {},
+            }
+
+        units = [unit_x1(0, (256, 256, 0, 256))]
+        units.extend([unit_x0(n) for n in range(4)])
+        units.append(unit_x1(1, (256, 256, 0, 256)))
+        units.append(unit_x2())
+        wprep_at = {0: 1, 1: 0, 3: 2}
+
+        count = len(units)
+        for i in range(count + 2):
+            u = units[i] if i < count else None
+            p1 = units[i - 1] if 1 <= i <= count else None
+            p2 = units[i - 2] if i >= 2 else None
+            if u is not None:
+                if u["lvl"] == 2:
+                    stage_r_x2(u, 0)
+                else:
+                    stage_r(u, 0)
+            if i in wprep_at:
+                wprep_a(wprep_at[i])
+            if p1 is not None:
+                stage_sg(p1)
+                stage_tr(p1)
+            if p2 is not None:
+                stage_bx(p2)
+                stage_st(p2)
+            if u is not None and len(u["chunks"]) > 1:
+                stage_r(u, 1)
+            if i in wprep_at:
+                wprep_b(wprep_at[i])
+            if u is not None:
+                stage_q(u, 0)
+            if p1 is not None:
+                stage_ev(p1)
+            if u is not None and len(u["chunks"]) > 1:
+                stage_q(u, 1)

@@ -16,7 +16,8 @@ ACT = mybir.ActivationFunctionType
 
 P = 128
 MANUAL = False
-WV0 = 648
+GI = 8
+WV0 = 640
 
 
 def tile_objectboxdetect_t_kernel(tc, x0, x1, x2, W0, b0, W1, b1, W2, b2, out):
@@ -173,13 +174,13 @@ def tile_objectboxdetect_t_kernel(tc, x0, x1, x2, W0, b0, W1, b1, W2, b2, out):
             width = dst.shape[1]
             if wv > 0:
                 nc.vector.tensor_copy(
-                    out=dst[:, 0:wv, :].rearrange("p (c i) t -> p c t i", i=4),
-                    in_=src[:, :, 0:wv].rearrange("p t (c i) -> p c t i", i=4),
+                    out=dst[:, 0:wv, :].rearrange("p (c i) t -> p c t i", i=GI),
+                    in_=src[:, :, 0:wv].rearrange("p t (c i) -> p c t i", i=GI),
                 )
             if wv < width:
                 nc.scalar.copy(
-                    out=dst[:, wv:width, :].rearrange("p (c i) t -> p c t i", i=4),
-                    in_=src[:, :, wv:width].rearrange("p t (c i) -> p c t i", i=4),
+                    out=dst[:, wv:width, :].rearrange("p (c i) t -> p c t i", i=GI),
+                    in_=src[:, :, wv:width].rearrange("p t (c i) -> p c t i", i=GI),
                 )
 
         def stage_r(u, k):
@@ -192,12 +193,12 @@ def tile_objectboxdetect_t_kernel(tc, x0, x1, x2, W0, b0, W1, b1, W2, b2, out):
         def stage_r_x2(u, k):
             grp = grpp.tile([P, 1024, 4], BF16, tag="grp", align_bytes=64)
             nc.vector.tensor_copy(
-                out=grp[:, 0:256, :].rearrange("p (n c i) t -> p n c t i", n=4, i=4),
-                in_=x2src[0].rearrange("p n t (c i) -> p n c t i", i=4),
+                out=grp[:, 0:256, :].rearrange("p (n c i) t -> p n c t i", n=4, i=GI),
+                in_=x2src[0].rearrange("p n t (c i) -> p n c t i", i=GI),
             )
             nc.vector.tensor_copy(
-                out=grp[:, 256:384, :].rearrange("p (n c i) t -> p n c t i", n=2, i=4),
-                in_=x2src[1][:, 0:2].rearrange("p n t (c i) -> p n c t i", i=4),
+                out=grp[:, 256:384, :].rearrange("p (n c i) t -> p n c t i", n=2, i=GI),
+                in_=x2src[1][:, 0:2].rearrange("p n t (c i) -> p n c t i", i=GI),
             )
             nc.scalar.copy(
                 out=grp[:, 384:512, :].rearrange("p (n w) t -> p n w t", n=2),

@@ -17,6 +17,8 @@ ACT = mybir.ActivationFunctionType
 P = 128
 MANUAL = False
 GI = 8
+WV1 = 160
+WV2 = 40
 WV0 = 640
 
 
@@ -38,7 +40,6 @@ def tile_objectboxdetect_t_kernel(tc, x0, x1, x2, W0, b0, W1, b1, W2, b2, out):
 
         x1src = {}
         x0src = {}
-        x2src = {}
         wraw = {}
 
         def load_x1_half(n, c):
@@ -66,13 +67,20 @@ def tile_objectboxdetect_t_kernel(tc, x0, x1, x2, W0, b0, W1, b1, W2, b2, out):
             )
             x0src[(n, c)] = t[:]
 
-        def load_x2(c):
-            t = rawp.tile([P, 4, 4, 64], BF16, name="x2_%d" % c)
+        x1b = rawp.tile([P, 2, 2, 4, 256], BF16, name="x1b")
+        x2t = rawp.tile([P, 2, 4, 4, 64], BF16, name="x2t")
+
+        def load_x1b(k):
             nc.sync.dma_start(
-                out=t[:].rearrange("p n j w -> p n (j w)"),
+                out=x1b[:, :, k].rearrange("p c j w -> p c (j w)"),
+                in_=x1[2 + k].rearrange("(c p j) h w -> p c (j h w)", c=2, j=4),
+            )
+
+        def load_x2(c):
+            nc.sync.dma_start(
+                out=x2t[:, c].rearrange("p n j w -> p n (j w)"),
                 in_=x2[:, 512 * c : 512 * (c + 1)].rearrange("n (p j) h w -> p n (j h w)", j=4),
             )
-            x2src[c] = t[:]
 
         def load_w(lvl):
             t = rawp.tile([P, 1024], BF16, name="w_%d" % lvl)
@@ -92,8 +100,8 @@ def tile_objectboxdetect_t_kernel(tc, x0, x1, x2, W0, b0, W1, b1, W2, b2, out):
         for n in range(2, 4):
             load_x0(n, 0)
             load_x0(n, 1)
-        load_x1(2)
-        load_x1(3)
+        load_x1b(0)
+        load_x1b(1)
         load_x2(0)
         load_x2(1)
 
@@ -109,23 +117,24 @@ def tile_objectboxdetect_t_kernel(tc, x0, x1, x2, W0, b0, W1, b1, W2, b2, out):
         warm2 = const.tile([P, 1], F32, name="warm2")
         nc.scalar.activation(out=warm2[:], in_=warm[:], func=ACT.Sigmoid)
 
-        idx = const.tile([P, 14], I32, name="idx")
+        idx = const.tile([P, 22], I32, name="idx")
         nc.gpsimd.iota(idx[:, 0:8], pattern=[[1, 8]], base=0, channel_multiplier=8)
         nc.gpsimd.iota(idx[:, 8:12], pattern=[[0, 2], [1, 2]], base=0, channel_multiplier=2)
         nc.gpsimd.iota(idx[:, 12:14], pattern=[[0, 2]], base=0, channel_multiplier=1)
+        nc.gpsimd.iota(idx[:, 14:22], pattern=[[512, 2], [1, 4]], base=0, channel_multiplier=4)
         ident = const.tile([P, P], F32, name="ident")
         make_identity(nc, ident[:])
 
-        gint = const.tile([P, 14, 2], I32, name="gint")
-        grid = const.tile([P, 14, 2], F32, name="grid")
-        slots = ((0, 8), (8, 12), (12, 14))
+        gint = const.tile([P, 22, 2], I32, name="gint")
+        grid = const.tile([P, 22, 2], F32, name="grid")
+        slots = ((0, 8), (8, 12), (12, 14), (14, 22))
         bits = (
             ((31, ALU.logical_shift_left, 3), (0x3E0, ALU.logical_shift_right, 2)),
             ((15, ALU.logical_shift_left, 4), (0xF0, ALU.logical_shift_left, 0)),
             ((7, ALU.logical_shift_left, 5), (56, ALU.logical_shift_left, 2)),
         )
-        for lvl in range(3):
-            lo, hi = slots[lvl]
+        for entry, lvl in enumerate((0, 1, 2, 0)):
+            lo, hi = slots[entry]
             for axis in range(2):
                 mask, shift_op, shift = bits[lvl][axis]
                 nc.vector.tensor_scalar(
@@ -190,19 +199,17 @@ def tile_objectboxdetect_t_kernel(tc, x0, x1, x2, W0, b0, W1, b1, W2, b2, out):
                 regroup(grp[:, lo : lo + width, :], src, wv)
             u["grp"][k] = grp
 
-        def stage_r_x2(u, k):
+        def stage_r_multi(u, k):
+            src4, blocks, width, wv = u["multi"]
             grp = grpp.tile([P, 1024, 4], BF16, tag="grp", align_bytes=64)
+            dst4 = grp[:, 0 : blocks * width, :].rearrange("p (s w) t -> p s w t", s=blocks)
             nc.vector.tensor_copy(
-                out=grp[:, 0:256, :].rearrange("p (n c i) t -> p n c t i", n=4, i=GI),
-                in_=x2src[0].rearrange("p n t (c i) -> p n c t i", i=GI),
-            )
-            nc.vector.tensor_copy(
-                out=grp[:, 256:384, :].rearrange("p (n c i) t -> p n c t i", n=2, i=GI),
-                in_=x2src[1][:, 0:2].rearrange("p n t (c i) -> p n c t i", i=GI),
+                out=dst4[:, :, 0:wv, :].rearrange("p s (c i) t -> p s c t i", i=GI),
+                in_=src4[:, :, :, 0:wv].rearrange("p s t (c i) -> p s c t i", i=GI),
             )
             nc.scalar.copy(
-                out=grp[:, 384:512, :].rearrange("p (n w) t -> p n w t", n=2),
-                in_=x2src[1][:, 2:4].rearrange("p n t w -> p n w t"),
+                out=dst4[:, :, wv:width, :].rearrange("p s (c i) t -> p s c t i", i=GI),
+                in_=src4[:, :, :, wv:width].rearrange("p s t (c i) -> p s c t i", i=GI),
             )
             u["grp"][k] = grp
 
@@ -236,7 +243,10 @@ def tile_objectboxdetect_t_kernel(tc, x0, x1, x2, W0, b0, W1, b1, W2, b2, out):
             u["y"] = y
             for bank in sorted(u["acc"]):
                 acc = u["acc"][bank]
-                if lvl == 0:
+                if lvl == 0 and u["local"]:
+                    dst = y[:, 4 * bank : 4 * bank + 4, :]
+                    src = acc[:].rearrange("o (m t) -> o t m", t=4)
+                elif lvl == 0:
                     dst = y[:, :, 64 * bank : 64 * bank + 64]
                     src = acc[:].rearrange("o (m t) -> o t m", t=8)
                 elif lvl == 1:
@@ -268,11 +278,57 @@ def tile_objectboxdetect_t_kernel(tc, x0, x1, x2, W0, b0, W1, b1, W2, b2, out):
                 else:
                     nc.scalar.copy(out=o[:, per * g : per * (g + 1), :], in_=zt[:, 0:per, :])
 
-        def stage_bx(u):
+        def stage_ev_fast(u):
+            nt = u["nt"]
+            zt = u["zt"][0]
+            o = outp.tile([P, nt, P], F32, name="o_" + u["name"])
+            u["o"] = o
+            qq = small.tile([P, 8, 4], F32, tag="q")
+            u["qq"] = qq
+            nc.scalar.activation(
+                out=qq[:, 0:nt, :], in_=zt[:, 0:nt, 0:4], func=ACT.Square, scale=float(4 << u["lvl"])
+            )
+            nc.scalar.copy(out=o[:, :, 4:P], in_=zt[:, 0:nt, 4:P])
+
+        def stage_bx_fast(u):
             lvl = u["lvl"]
             nt = u["nt"]
             o = u["o"]
+            qq = u["qq"]
             lo = slots[lvl][0]
+            stride = float(8 << lvl)
+            e = small.tile([P, 8, 2], F32, tag="d")
+            g = small.tile([P, 8, 2], F32, tag="s")
+            nc.vector.scalar_tensor_tensor(
+                out=e[:, 0:nt, :],
+                in0=qq[:, 0:nt, 0:2],
+                scalar=-1.0,
+                in1=grid[:, lo : lo + nt, :],
+                op0=ALU.mult,
+                op1=ALU.add,
+            )
+            nc.vector.tensor_scalar(
+                out=g[:, 0:nt, :],
+                in0=qq[:, 0:nt, 0:2],
+                scalar1=2.0,
+                scalar2=-stride,
+                op0=ALU.mult,
+                op1=ALU.add,
+            )
+            nc.vector.tensor_tensor(out=o[:, :, 0:2], in0=qq[:, 0:nt, 2:4], in1=e[:, 0:nt, :], op=ALU.add)
+            nc.vector.scalar_tensor_tensor(
+                out=o[:, :, 2:4],
+                in0=qq[:, 0:nt, 2:4],
+                scalar=2.0,
+                in1=g[:, 0:nt, :],
+                op0=ALU.mult,
+                op1=ALU.add,
+            )
+
+        def stage_bx(u, first, nt):
+            lvl = u["lvl"]
+            o = u["o"][:, first : first + nt, :]
+            lo = slots[3 if u["local"] else lvl][0] + first
             stride = float(8 << lvl)
             power = float(1 << lvl)
             q = small.tile([P, 8, 4], F32, tag="q")
@@ -300,6 +356,12 @@ def tile_objectboxdetect_t_kernel(tc, x0, x1, x2, W0, b0, W1, b1, W2, b2, out):
                 scalar2=-stride,
                 op0=ALU.mult,
                 op1=ALU.add,
+            )
+
+        def stage_st_half(u, h):
+            nc.sync.dma_start(
+                out=out[u["n"], 512 * h : 512 * h + 512, :].rearrange("(m t) o -> m (t o)", t=4),
+                in_=u["o"][:, 4 * h : 4 * h + 4, :].rearrange("m t o -> m (t o)"),
             )
 
         def stage_st(u):
@@ -332,6 +394,7 @@ def tile_objectboxdetect_t_kernel(tc, x0, x1, x2, W0, b0, W1, b1, W2, b2, out):
                 "per_bank": 4,
                 "ev": ["s", "s"],
                 "grp": {},
+                "local": False,
                 "acc": {},
             }
 
@@ -350,26 +413,47 @@ def tile_objectboxdetect_t_kernel(tc, x0, x1, x2, W0, b0, W1, b1, W2, b2, out):
                 "per_bank": 4,
                 "ev": ["s"],
                 "grp": {},
+                "local": False,
+                "acc": {},
+            }
+
+        def unit_x1b():
+            return {
+                "name": "l11",
+                "lvl": 1,
+                "n": 2,
+                "multi": (x1b[:].rearrange("p c k j w -> p (c k) j w"), 4, 256, WV1),
+                "chunks": [(1024, None)],
+                "mx": [[(0, c, 512 * c, 512) for c in range(2)]],
+                "nt": 4,
+                "per_bank": 4,
+                "ev": ["s"],
+                "grp": {},
+                "local": False,
                 "acc": {},
             }
 
         def unit_x2():
             return {
                 "name": "l2",
+                "multi": (x2t[:].rearrange("p c n j w -> p (c n) j w"), 8, 64, WV2),
                 "lvl": 2,
                 "n": 0,
                 "chunks": [(512, None)],
                 "mx": [[(0, c, 256 * c, 256) for c in range(2)]],
                 "nt": 2,
-                "per_bank": 1,
-                "ev": ["v", "s"],
+                "per_bank": 2,
+                "ev": ["s"],
+                "fast": True,
                 "grp": {},
+                "local": False,
                 "acc": {},
             }
 
         units = [unit_x1(0, (256, 256, 0, 256))]
         units.extend([unit_x0(n) for n in range(4)])
-        units.append(unit_x1(1, (256, 256, 0, 256)))
+        units[4]["local"] = True
+        units.append(unit_x1b())
         units.append(unit_x2())
         wprep_at = {0: 1, 1: 0, 3: 2}
 
@@ -379,8 +463,8 @@ def tile_objectboxdetect_t_kernel(tc, x0, x1, x2, W0, b0, W1, b1, W2, b2, out):
             p1 = units[i - 1] if 1 <= i <= count else None
             p2 = units[i - 2] if i >= 2 else None
             if u is not None:
-                if u["lvl"] == 2:
-                    stage_r_x2(u, 0)
+                if "multi" in u:
+                    stage_r_multi(u, 0)
                 else:
                     stage_r(u, 0)
             if i in wprep_at:
@@ -389,8 +473,16 @@ def tile_objectboxdetect_t_kernel(tc, x0, x1, x2, W0, b0, W1, b1, W2, b2, out):
                 stage_sg(p1)
                 stage_tr(p1)
             if p2 is not None:
-                stage_bx(p2)
-                stage_st(p2)
+                if "fast" in p2:
+                    stage_bx_fast(p2)
+                    stage_st(p2)
+                elif p2["local"]:
+                    for h in range(2):
+                        stage_bx(p2, 4 * h, 4)
+                        stage_st_half(p2, h)
+                else:
+                    stage_bx(p2, 0, p2["nt"])
+                    stage_st(p2)
             if u is not None and len(u["chunks"]) > 1:
                 stage_r(u, 1)
             if i in wprep_at:
@@ -398,6 +490,9 @@ def tile_objectboxdetect_t_kernel(tc, x0, x1, x2, W0, b0, W1, b1, W2, b2, out):
             if u is not None:
                 stage_q(u, 0)
             if p1 is not None:
-                stage_ev(p1)
+                if "fast" in p1:
+                    stage_ev_fast(p1)
+                else:
+                    stage_ev(p1)
             if u is not None and len(u["chunks"]) > 1:
                 stage_q(u, 1)

@@ -428,6 +428,7 @@ def tile_objectboxdetect_t_kernel(tc, x0, x1, x2, W0, b0, W1, b1, W2, b2, out):
                 "nt": 4,
                 "per_bank": 4,
                 "ev": ["s"],
+                "fast": True,
                 "grp": {},
                 "local": False,
                 "acc": {},

from contextlib import ExitStack

import concourse.mybir as mybir
from concourse.masks import make_identity

FLOPS = 2 * 4 * 1344 * 1024 * 128

BF16 = mybir.dt.bfloat16
F32 = mybir.dt.float32
I32 = mybir.dt.int32
U32 = mybir.dt.uint32
U8 = mybir.dt.uint8
FP8X4 = mybir.dt.float8_e4m3fn_x4
ALU = mybir.AluOpType
ACT = mybir.ActivationFunctionType

P = 128
MANUAL = False
GI = 8
WV1 = 160
WV2 = 40
WV0 = 640


def tile_objectboxdetect_t_kernel(tc, x0, x1, x2, W0, b0, W1, b1, W2, b2, out):
    nc = tc.nc
    weights = (W0, W1, W2)
    biases = (b0, b1, b2)
    with ExitStack() as ctx:
        if MANUAL:
            ctx.enter_context(tc.manual_schedule())
        const = ctx.enter_context(tc.tile_pool(name="const", bufs=1))
        rawp = ctx.enter_context(tc.tile_pool(name="raw", bufs=1))
        grpp = ctx.enter_context(tc.tile_pool(name="grp", bufs=4))
        codep = ctx.enter_context(tc.tile_pool(name="code", bufs=6))
        yp = ctx.enter_context(tc.tile_pool(name="y", bufs=3))
        outp = ctx.enter_context(tc.tile_pool(name="o", bufs=1))
        small = ctx.enter_context(tc.tile_pool(name="small", bufs=3))
        psum = ctx.enter_context(tc.psum_pool(name="psum", bufs=4))

        x1src = {}
        x0src = {}
        wraw = {}

        def load_x1_half(n, c):
            t = rawp.tile([P, 4, 256], BF16, name="x1_%d_%d" % (n, c))
            nc.sync.dma_start(
                out=t[:].rearrange("p j w -> p (j w)"),
                in_=x1[n, 512 * c : 512 * (c + 1)].rearrange("(p j) h w -> p (j h w)", j=4),
            )
            x1src[(n, c)] = t[:]

        def load_x1(n):
            t = rawp.tile([P, 2, 4, 256], BF16, name="x1_%d" % n)
            nc.sync.dma_start(
                out=t[:].rearrange("p c j w -> p c (j w)"),
                in_=x1[n].rearrange("(c p j) h w -> p c (j h w)", c=2, j=4),
            )
            x1src[(n, 0)] = t[:, 0]
            x1src[(n, 1)] = t[:, 1]

        def load_x0(n, c):
            t = rawp.tile([P, 4, 1024], BF16, name="x0_%d_%d" % (n, c))
            nc.sync.dma_start(
                out=t[:].rearrange("p j w -> p (j w)"),
                in_=x0[n, 512 * c : 512 * (c + 1)].rearrange("(p j) h w -> p (j h w)", j=4),
            )
            x0src[(n, c)] = t[:]

        x1b = rawp.tile([P, 2, 2, 4, 256], BF16, name="x1b")
        x2t = rawp.tile([P, 2, 4, 4, 64], BF16, name="x2t")

        def load_x1b(k):
            nc.sync.dma_start(
                out=x1b[:, :, k].rearrange("p c j w -> p c (j w)"),
                in_=x1[2 + k].rearrange("(c p j) h w -> p c (j h w)", c=2, j=4),
            )

        def load_x2(c):
            nc.sync.dma_start(
                out=x2t[:, c].rearrange("p n j w -> p n (j w)"),
                in_=x2[:, 512 * c : 512 * (c + 1)].rearrange("n (p j) h w -> p n (j h w)", j=4),
            )

        def load_w(lvl):
            t = rawp.tile([P, 1024], BF16, name="w_%d" % lvl)
            nc.sync.dma_start(out=t[:], in_=weights[lvl][:, :])
            wraw[lvl] = t

        load_x1_half(0, 0)
        load_w(1)
        load_x1_half(0, 1)
        load_x1(1)
        load_x0(0, 0)
        load_w(0)
        load_x0(0, 1)
        load_x0(1, 0)
        load_w(2)
        load_x0(1, 1)
        for n in range(2, 4):
            load_x0(n, 0)
            load_x0(n, 1)
        load_x1b(0)
        load_x1b(1)
        load_x2(0)
        load_x2(1)

        bias_bf = []
        with nc.allow_non_contiguous_dma(reason="128 two-byte values, one a partition"):
            for lvl in range(3):
                t = const.tile([P, 1], BF16, name="bias_bf_%d" % lvl)
                nc.scalar.dma_start(out=t[:], in_=biases[lvl].rearrange("(p o) -> p o", o=1))
                bias_bf.append(t)

        warm = const.tile([P, 1], F32, name="warm")
        nc.vector.memset(warm[:], 0.0)
        warm2 = const.tile([P, 1], F32, name="warm2")
        nc.scalar.activation(out=warm2[:], in_=warm[:], func=ACT.Sigmoid)

        idx = const.tile([P, 22], I32, name="idx")
        nc.gpsimd.iota(idx[:, 0:8], pattern=[[1, 8]], base=0, channel_multiplier=8)
        nc.gpsimd.iota(idx[:, 8:12], pattern=[[0, 2], [1, 2]], base=0, channel_multiplier=2)
        nc.gpsimd.iota(idx[:, 12:14], pattern=[[0, 2]], base=0, channel_multiplier=1)
        nc.gpsimd.iota(idx[:, 14:22], pattern=[[512, 2], [1, 4]], base=0, channel_multiplier=4)
        ident = const.tile([P, P], F32, name="ident")
        make_identity(nc, ident[:])

        gint = const.tile([P, 22, 2], I32, name="gint")
        grid = const.tile([P, 22, 2], F32, name="grid")
        slots = ((0, 8), (8, 12), (12, 14), (14, 22))
        bits = (
            ((31, ALU.logical_shift_left, 3), (0x3E0, ALU.logical_shift_right, 2)),
            ((15, ALU.logical_shift_left, 4), (0xF0, ALU.logical_shift_left, 0)),
            ((7, ALU.logical_shift_left, 5), (56, ALU.logical_shift_left, 2)),
        )
        for entry, lvl in enumerate((0, 1, 2, 0)):
            lo, hi = slots[entry]
            for axis in range(2):
                mask, shift_op, shift = bits[lvl][axis]
                nc.vector.tensor_scalar(
                    out=gint[:, lo:hi, axis],
                    in0=idx[:, lo:hi],
                    scalar1=mask,
                    scalar2=shift,
                    op0=ALU.bitwise_and,
                    op1=shift_op,
                )
            nc.vector.tensor_scalar(
                out=grid[:, lo:hi, :],
                in0=gint[:, lo:hi, :],
                scalar1=float(4 << lvl),
                scalar2=None,
                op0=ALU.add,
            )

        bias = const.tile([P, 3], F32, name="bias")
        wcodes = {}
        wscales = {}
        wgrouped = {}

        def wprep_a(lvl):
            nc.vector.tensor_copy(out=bias[:, lvl : lvl + 1], in_=bias_bf[lvl][:])
            words = wraw[lvl][:].bitcast(F32).rearrange("o (c p u) -> o c u p", c=2, u=2)
            wt = psum.tile([P, 2, 2, P], F32, tag="zt")
            for c in range(2):
                for u in range(2):
                    nc.tensor.transpose(wt[:, c, u, :], words[:, c, u, :], ident[:])
            wg = const.tile([P, 1024], BF16, name="wg_%d" % lvl, align_bytes=64)
            nc.scalar.copy(
                out=wg[:].bitcast(F32).rearrange("p (c o u) -> p c o u", c=2, u=2),
                in_=wt[:].rearrange("p c u o -> p c o u"),
            )
            wgrouped[lvl] = wg

        def wprep_b(lvl):
            wc = const.tile([P, 256], U32, name="wc_%d" % lvl, align_bytes=64)
            ws = const.tile([P, 256], U8, name="ws_%d" % lvl, align_bytes=64)
            nc.vector.quantize_mx(out=wc[:].bitcast(FP8X4), scales=ws[:], in_=wgrouped[lvl][:])
            wcodes[lvl] = wc
            wscales[lvl] = ws

        def regroup(dst, src, wv):
            width = dst.shape[1]
            if wv > 0:
                nc.vector.tensor_copy(
                    out=dst[:, 0:wv, :].rearrange("p (c i) t -> p c t i", i=GI),
                    in_=src[:, :, 0:wv].rearrange("p t (c i) -> p c t i", i=GI),
                )
            if wv < width:
                nc.scalar.copy(
                    out=dst[:, wv:width, :].rearrange("p (c i) t -> p c t i", i=GI),
                    in_=src[:, :, wv:width].rearrange("p t (c i) -> p c t i", i=GI),
                )

        def stage_r(u, k):
            words, subs = u["chunks"][k]
            grp = grpp.tile([P, 1024, 4], BF16, tag="grp", align_bytes=64)
            for lo, width, src, wv in subs:
                regroup(grp[:, lo : lo + width, :], src, wv)
            u["grp"][k] = grp

        def stage_r_multi(u, k):
            src4, blocks, width, wv = u["multi"]
            grp = grpp.tile([P, 1024, 4], BF16, tag="grp", align_bytes=64)
            dst4 = grp[:, 0 : blocks * width, :].rearrange("p (s w) t -> p s w t", s=blocks)
            nc.vector.tensor_copy(
                out=dst4[:, :, 0:wv, :].rearrange("p s (c i) t -> p s c t i", i=GI),
                in_=src4[:, :, :, 0:wv].rearrange("p s t (c i) -> p s c t i", i=GI),
            )
            nc.scalar.copy(
                out=dst4[:, :, wv:width, :].rearrange("p s (c i) t -> p s c t i", i=GI),
                in_=src4[:, :, :, wv:width].rearrange("p s t (c i) -> p s c t i", i=GI),
            )
            u["grp"][k] = grp

        def stage_q(u, k):
            words = u["chunks"][k][0]
            lvl = u["lvl"]
            codes = codep.tile([P, 1024], U32, tag="codes", align_bytes=64)
            scl = codep.tile([P, 1024], U8, tag="scl", align_bytes=64)
            nc.vector.quantize_mx(
                out=codes[:, 0:words].bitcast(FP8X4),
                scales=scl[:, 0:words],
                in_=u["grp"][k][:, 0:words, :].rearrange("p w t -> p (w t)"),
            )
            for bank, c, lo, cols in u["mx"][k]:
                if c == 0:
                    acc = psum.tile([P, 512], F32, tag="acc")
                    u["acc"][bank] = acc
                nc.tensor.matmul_mx(
                    out=u["acc"][bank][:, 0:cols],
                    lhsT=wcodes[lvl][:, P * c : P * (c + 1)].bitcast(FP8X4),
                    lhsT_scale=wscales[lvl][:, P * c : P * (c + 1)],
                    rhs=codes[:, lo : lo + cols].bitcast(FP8X4),
                    rhs_scale=scl[:, lo : lo + cols],
                    start=(c == 0),
                    stop=(c == 1),
                )

        def stage_sg(u):
            lvl = u["lvl"]
            y = yp.tile([P, 8, P], F32, tag="y")
            u["y"] = y
            for bank in sorted(u["acc"]):
                acc = u["acc"][bank]
                if lvl == 0 and u["local"]:
                    dst = y[:, 4 * bank : 4 * bank + 4, :]
                    src = acc[:].rearrange("o (m t) -> o t m", t=4)
                elif lvl == 0:
                    dst = y[:, :, 64 * bank : 64 * bank + 64]
                    src = acc[:].rearrange("o (m t) -> o t m", t=8)
                elif lvl == 1:
                    dst = y[:, 0:4, :].rearrange("o (n t) m -> o n t m", n=2)
                    src = acc[:].rearrange("o (n m t) -> o n t m", n=2, t=2)
                else:
                    dst = y[:, 0:2, :].rearrange("o g m -> o (g m)")
                    src = acc[:, 0:256]
                nc.scalar.activation(
                    out=dst, in_=src, func=ACT.Sigmoid, bias=bias[:, lvl : lvl + 1], scale=1.0
                )

        def stage_tr(u):
            u["zt"] = []
            per = u["per_bank"]
            for g in range(u["nt"] // per):
                zt = psum.tile([P, 4, P], F32, tag="zt")
                for s in range(per):
                    nc.tensor.transpose(zt[:, s, :], u["y"][:, per * g + s, :], ident[:])
                u["zt"].append(zt)

        def stage_ev(u):
            per = u["per_bank"]
            o = outp.tile([P, u["nt"], P], F32, name="o_" + u["name"])
            u["o"] = o
            for g, zt in enumerate(u["zt"]):
                if u["ev"][g] == "v":
                    nc.vector.tensor_copy(out=o[:, per * g : per * (g + 1), :], in_=zt[:, 0:per, :])
                else:
                    nc.scalar.copy(out=o[:, per * g : per * (g + 1), :], in_=zt[:, 0:per, :])

        def stage_ev_fast(u):
            nt = u["nt"]
            zt = u["zt"][0]
            o = outp.tile([P, nt, P], F32, name="o_" + u["name"])
            u["o"] = o
            qq = small.tile([P, 8, 4], F32, tag="q")
            u["qq"] = qq
            nc.scalar.activation(
                out=qq[:, 0:nt, :], in_=zt[:, 0:nt, 0:4], func=ACT.Square, scale=float(4 << u["lvl"])
            )
            nc.scalar.copy(out=o[:, :, 4:P], in_=zt[:, 0:nt, 4:P])

        def stage_bx_fast(u):
            lvl = u["lvl"]
            nt = u["nt"]
            o = u["o"]
            qq = u["qq"]
            lo = slots[lvl][0]
            stride = float(8 << lvl)
            e = small.tile([P, 8, 2], F32, tag="d")
            g = small.tile([P, 8, 2], F32, tag="s")
            nc.vector.scalar_tensor_tensor(
                out=e[:, 0:nt, :],
                in0=qq[:, 0:nt, 0:2],
                scalar=-1.0,
                in1=grid[:, lo : lo + nt, :],
                op0=ALU.mult,
                op1=ALU.add,
            )
            nc.vector.tensor_scalar(
                out=g[:, 0:nt, :],
                in0=qq[:, 0:nt, 0:2],
                scalar1=2.0,
                scalar2=-stride,
                op0=ALU.mult,
                op1=ALU.add,
            )
            nc.vector.tensor_tensor(out=o[:, :, 0:2], in0=qq[:, 0:nt, 2:4], in1=e[:, 0:nt, :], op=ALU.add)
            nc.vector.scalar_tensor_tensor(
                out=o[:, :, 2:4],
                in0=qq[:, 0:nt, 2:4],
                scalar=2.0,
                in1=g[:, 0:nt, :],
                op0=ALU.mult,
                op1=ALU.add,
            )

        def stage_bx(u, first, nt):
            lvl = u["lvl"]
            o = u["o"][:, first : first + nt, :]
            lo = slots[3 if u["local"] else lvl][0] + first
            stride = float(8 << lvl)
            power = float(1 << lvl)
            q = small.tile([P, 8, 4], F32, tag="q")
            d = small.tile([P, 8, 2], F32, tag="d")
            s = small.tile([P, 8, 2], F32, tag="s")
            nc.vector.tensor_tensor(out=q[:, 0:nt, :], in0=o[:, :, 0:4], in1=o[:, :, 0:4], op=ALU.mult)
            nc.vector.tensor_tensor(
                out=d[:, 0:nt, :], in0=q[:, 0:nt, 2:4], in1=q[:, 0:nt, 0:2], op=ALU.subtract
            )
            nc.vector.tensor_tensor(
                out=s[:, 0:nt, :], in0=q[:, 0:nt, 2:4], in1=q[:, 0:nt, 0:2], op=ALU.add
            )
            nc.vector.scalar_tensor_tensor(
                out=o[:, :, 0:2],
                in0=d[:, 0:nt, :],
                scalar=2.0 * power * stride,
                in1=grid[:, lo : lo + nt, :],
                op0=ALU.mult,
                op1=ALU.add,
            )
            nc.vector.tensor_scalar(
                out=o[:, :, 2:4],
                in0=s[:, 0:nt, :],
                scalar1=4.0 * power * stride,
                scalar2=-stride,
                op0=ALU.mult,
                op1=ALU.add,
            )

        def stage_st_half(u, h):
            nc.sync.dma_start(
                out=out[u["n"], 512 * h : 512 * h + 512, :].rearrange("(m t) o -> m (t o)", t=4),
                in_=u["o"][:, 4 * h : 4 * h + 4, :].rearrange("m t o -> m (t o)"),
            )

        def stage_st(u):
            o = u["o"]
            lvl = u["lvl"]
            if lvl == 0:
                nc.sync.dma_start(
                    out=out[u["n"], 0:1024, :].rearrange("(m t) o -> m (t o)", t=8),
                    in_=o[:].rearrange("m t o -> m (t o)"),
                )
            elif lvl == 1:
                n = u["n"]
                nc.sync.dma_start(
                    out=out[n : n + 2, 1024:1280, :].rearrange("n (m t) o -> m n (t o)", t=2),
                    in_=o[:].rearrange("m (n t) o -> m n (t o)", n=2),
                )
            else:
                for n in range(4):
                    half = 64 * (n % 2)
                    nc.sync.dma_start(out=out[n, 1280:1344, :], in_=o[half : half + 64, n // 2, :])

        def unit_x0(n):
            return {
                "name": "b%d" % n,
                "lvl": 0,
                "n": n,
                "chunks": [(1024, [(0, 1024, x0src[(n, c)], WV0)]) for c in range(2)],
                "mx": [[(h, c, 512 * h, 512) for h in range(2)] for c in range(2)],
                "nt": 8,
                "per_bank": 4,
                "ev": ["s", "s"],
                "grp": {},
                "local": False,
                "acc": {},
            }

        def unit_x1(h, wvs):
            subs = []
            for c in range(2):
                for k in range(2):
                    subs.append((512 * c + 256 * k, 256, x1src[(2 * h + k, c)], wvs[2 * c + k]))
            return {
                "name": "l1%d" % h,
                "lvl": 1,
                "n": 2 * h,
                "chunks": [(1024, subs)],
                "mx": [[(0, c, 512 * c, 512) for c in range(2)]],
                "nt": 4,
                "per_bank": 4,
                "ev": ["s"],
                "grp": {},
                "local": False,
                "acc": {},
            }

        def unit_x1b():
            return {
                "name": "l11",
                "lvl": 1,
                "n": 2,
                "multi": (x1b[:].rearrange("p c k j w -> p (c k) j w"), 4, 256, WV1),
                "chunks": [(1024, None)],
                "mx": [[(0, c, 512 * c, 512) for c in range(2)]],
                "nt": 4,
                "per_bank": 4,
                "ev": ["s"],
                "fast": True,
                "grp": {},
                "local": False,
                "acc": {},
            }

        def unit_x2():
            return {
                "name": "l2",
                "multi": (x2t[:].rearrange("p c n j w -> p (c n) j w"), 8, 64, WV2),
                "lvl": 2,
                "n": 0,
                "chunks": [(512, None)],
                "mx": [[(0, c, 256 * c, 256) for c in range(2)]],
                "nt": 2,
                "per_bank": 2,
                "ev": ["s"],
                "fast": True,
                "grp": {},
                "local": False,
                "acc": {},
            }

        units = [unit_x1(0, (256, 256, 0, 256))]
        units.extend([unit_x0(n) for n in range(4)])
        units[4]["local"] = True
        units.append(unit_x1b())
        units.append(unit_x2())
        wprep_at = {0: 1, 1: 0, 3: 2}

        count = len(units)
        for i in range(count + 2):
            u = units[i] if i < count else None
            p1 = units[i - 1] if 1 <= i <= count else None
            p2 = units[i - 2] if i >= 2 else None
            if u is not None:
                if "multi" in u:
                    stage_r_multi(u, 0)
                else:
                    stage_r(u, 0)
            if i in wprep_at:
                wprep_a(wprep_at[i])
            if p1 is not None:
                stage_sg(p1)
                stage_tr(p1)
            if p2 is not None:
                if "fast" in p2:
                    stage_bx_fast(p2)
                    stage_st(p2)
                elif p2["local"]:
                    for h in range(2):
                        stage_bx(p2, 4 * h, 4)
                        stage_st_half(p2, h)
                else:
                    stage_bx(p2, 0, p2["nt"])
                    stage_st(p2)
            if u is not None and len(u["chunks"]) > 1:
                stage_r(u, 1)
            if i in wprep_at:
                wprep_b(wprep_at[i])
            if u is not None:
                stage_q(u, 0)
            if p1 is not None:
                if "fast" in p1:
                    stage_ev_fast(p1)
                else:
                    stage_ev(p1)
            if u is not None and len(u["chunks"]) > 1:
                stage_q(u, 1)
